import numpy as np
import ml_dtypes


def mxq(x, axis, fmt="e4m3"):
    dtype, down = {"e4m3": (ml_dtypes.float8_e4m3fn, 7), "e5m2": (ml_dtypes.float8_e5m2, 14)}[fmt]
    v = np.moveaxis(np.asarray(x, np.float32).astype(ml_dtypes.bfloat16).astype(np.float64), axis, -1)
    blocks = v.reshape(v.shape[:-1] + (-1, 32))
    amax = np.abs(blocks).max(-1, keepdims=True)
    byte = np.maximum(np.where(amax > 0, np.frexp(amax)[1] - 1 + 127, 0) - down, 1)
    scale = np.exp2(byte - 127.0)
    codes = (blocks / scale).astype(np.float32).astype(dtype).astype(np.float64)
    return np.moveaxis((codes * scale).reshape(v.shape), -1, axis)


WIDE = False


def mx_kscale(k):
    if not WIDE:
        return np.ones(k)
    levels = np.array([10, -10, 5, -5, 0])
    a = np.random.permutation(np.resize(levels, k // 512 * 4)).reshape(k // 512, 4)
    idx = np.arange(k)
    return np.exp2(a[idx // 512, idx % 128 // 32])


BF16 = ml_dtypes.bfloat16


def bf(x):
    return np.asarray(x, np.float32).astype(BF16)


def f64(x):
    return np.asarray(x).astype(np.float64)


M, I0, I1, I2, N0, N1, N2 = 512, 1024, 2048, 4096, 1024, 1024, 2048


def block(fan_in, fan_out, s):
    return bf(np.random.uniform(-1.0, 1.0, (fan_in, fan_out)) / np.sqrt(fan_in) / s[:fan_in, None])


def setup_inputs():
    s = mx_kscale(I2)
    return {"x": bf(np.random.standard_normal((M, I2)) * s),
            "w0": block(I0, N0, s), "w1": block(I1, N1, s), "w2": block(I2, N2, s),
            "bias": bf(np.random.standard_normal(N0 + N1 + N2) * 0.1)}


def reference(x, w0, w1, w2, bias):
    xq = mxq(f64(x), 1, "e4m3")
    y0 = xq[:, :I0] @ mxq(f64(w0), 0, "e4m3")
    y1 = xq[:, :I1] @ mxq(f64(w1), 0, "e4m3")
    y2 = xq[:, :I2] @ mxq(f64(w2), 0, "e4m3")
    return np.concatenate([y0, y1, y2], axis=1) + f64(bias)

@@ -1,0 +1,235 @@
+from contextlib import ExitStack
+
+import concourse.mybir as mybir
+from concourse.masks import make_identity
+
+FP8X4 = mybir.dt.float8_e4m3fn_x4
+BF16 = mybir.dt.bfloat16
+F32 = mybir.dt.float32
+U32 = mybir.dt.uint32
+U8 = mybir.dt.uint8
+ADD = mybir.AluOpType.add
+
+P = 128
+M_TILES = 4
+K_PASS = 512
+UNIT_COLS = 1024
+BANK = 512
+FLOPS = 2 * 512 * (1024 * 1024 + 2048 * 1024 + 4096 * 2048)
+
+MANUAL = True
+RAW_BUFS = 12
+ROUND_SCALAR_COLS = (896, 704, 624, 512)
+
+
+def tile_mlinear_kernel(tc, x, w0, w1, w2, bias, out):
+    nc = tc.nc
+    with ExitStack() as ctx:
+        if MANUAL:
+            ctx.enter_context(tc.manual_schedule())
+        const = ctx.enter_context(tc.tile_pool(name="const", bufs=1))
+        rawp = ctx.enter_context(tc.tile_pool(name="rawp", bufs=RAW_BUFS))
+        grpp = ctx.enter_context(tc.tile_pool(name="grpp", bufs=4))
+        wqp = ctx.enter_context(tc.tile_pool(name="wqp", bufs=4))
+        stgp = ctx.enter_context(tc.tile_pool(name="stgp", bufs=6))
+        psum = ctx.enter_context(tc.psum_pool(name="psum", bufs=1))
+
+        units = []
+        rnd = 0
+        for w, k_len, n_len, o_col in ((w0, 1024, 1024, 0), (w1, 2048, 1024, 1024), (w2, 4096, 2048, 2048)):
+            for h in range(n_len // UNIT_COLS):
+                for c in range(k_len // K_PASS):
+                    units.append(
+                        (w, c, UNIT_COLS * h, o_col + UNIT_COLS * h, c == 0, c == k_len // K_PASS - 1, rnd)
+                    )
+                rnd += 1
+        n_units = len(units)
+
+        ident = const.tile([P, P], F32, name="ident")
+        identb = const.tile([P, P], BF16, name="identb")
+        brow = const.tile([P, BANK], BF16, name="brow")
+        bias_bc = const.tile([P, 4096], BF16, name="bias_bc")
+        xc = const.tile([P, M_TILES, 8, P], U32, name="xc", align_bytes=64)
+        xs = const.tile([P, M_TILES, 8, P], U8, name="xs", align_bytes=64)
+
+        raw = {}
+        grp = {}
+        wc = {}
+        ws = {}
+        acc = {}
+
+        def load_x(i):
+            t = rawp.tile([P, 4, 1024], BF16, name="raw", tag="raw")
+            raw[("x", i)] = t
+            rows = x[P * i : P * i + P, :].rearrange("p (b k) -> p b k", b=4)
+            if i == 0:
+                for b in range(4):
+                    nc.sync.dma_start(out=t[:, b, :], in_=rows[:, b, :])
+            else:
+                nc.sync.dma_start(out=t[:], in_=rows)
+
+        def load_w(u):
+            w, c, col = units[u][0:3]
+            t = rawp.tile([P, 4, 1024], BF16, name="raw", tag="raw")
+            raw[("w", u)] = t
+            for half in range(2):
+                r0 = K_PASS * c + 256 * half
+                nc.sync.dma_start(
+                    out=t[:, 2 * half : 2 * half + 2, :],
+                    in_=w[r0 : r0 + 256, col : col + UNIT_COLS].rearrange("(q e) n -> q e n", e=2),
+                )
+
+        def regroup(u):
+            t = raw[("w", u)]
+            g = grpp.tile([P, 4096], BF16, name="grp", tag="grp", align_bytes=64)
+            grp[u] = g
+            g3 = g[:].rearrange("p (n t) -> p n t", t=4)
+            cs = ROUND_SCALAR_COLS[units[u][6]]
+            nc.scalar.copy(
+                out=g3[:, 0:cs, :].rearrange("p (c i) t -> p c t i", i=4),
+                in_=t[:, :, 0:cs].rearrange("p t (c i) -> p c t i", i=4),
+            )
+            nc.vector.tensor_copy(
+                out=g3[:, cs:UNIT_COLS, :].rearrange("p (c i) t -> p c t i", i=4),
+                in_=t[:, :, cs:UNIT_COLS].rearrange("p t (c i) -> p c t i", i=4),
+            )
+
+        def quantise(u):
+            codes = wqp.tile([P, UNIT_COLS], U32, name="wc", tag="wc", align_bytes=64)
+            scales = wqp.tile([P, UNIT_COLS], U8, name="ws", tag="ws", align_bytes=64)
+            wc[u] = codes
+            ws[u] = scales
+            pieces = 2 if u == n_units - 1 else 1
+            wid = UNIT_COLS // pieces
+            for a in range(pieces):
+                nc.vector.quantize_mx(
+                    out=codes[:, wid * a : wid * a + wid].bitcast(FP8X4),
+                    scales=scales[:, wid * a : wid * a + wid],
+                    in_=grp[u][:, 4 * wid * a : 4 * wid * a + 4 * wid],
+                )
+
+        def bank_order(u):
+            if units[u][6] == rnd - 1:
+                return [(i, j) for j in range(2) for i in range(M_TILES)]
+            return [(i, j) for i in range(M_TILES) for j in range(2)]
+
+        def multiply(u):
+            c, first, last = units[u][1], units[u][4], units[u][5]
+            for i, j in bank_order(u):
+                b = 2 * i + j
+                if first:
+                    acc[b] = psum.tile([P, BANK], F32, name="acc%d" % b, tag="b%d" % b)
+                nc.tensor.matmul_mx(
+                    out=acc[b][:],
+                    lhsT=xc[:, i, c, :].bitcast(FP8X4),
+                    lhsT_scale=xs[:, i, c, :],
+                    rhs=wc[u][:, BANK * j : BANK * j + BANK].bitcast(FP8X4),
+                    rhs_scale=ws[u][:, BANK * j : BANK * j + BANK],
+                    start=first,
+                    stop=last,
+                )
+
+        def finish(u):
+            o_col = units[u][3]
+            fine = units[u][6] == rnd - 1
+            stg = {}
+            for i in range(M_TILES):
+                stg[i] = stgp.tile([P, UNIT_COLS], F32, name="stg", tag="stg")
+            for i, j in bank_order(u):
+                lo = BANK * j
+                nc.vector.tensor_tensor(
+                    out=stg[i][:, lo : lo + BANK],
+                    in0=acc[2 * i + j][:],
+                    in1=bias_bc[:, o_col + lo : o_col + lo + BANK],
+                    op=ADD,
+                )
+                if fine:
+                    nc.sync.dma_start(
+                        out=out[P * i : P * i + P, o_col + lo : o_col + lo + BANK], in_=stg[i][:, lo : lo + BANK]
+                    )
+                elif j == 1:
+                    nc.sync.dma_start(out=out[P * i : P * i + P, o_col : o_col + UNIT_COLS], in_=stg[i][:])
+
+        nc.vector.memset(brow[:], 0.0)
+        make_identity(nc, ident[:])
+        make_identity(nc, identb[:])
+        load_x(0)
+        nc.sync.dma_start(out=brow[0:8, :], in_=bias.rearrange("(c n) -> c n", c=8))
+        for i in range(1, M_TILES):
+            load_x(i)
+        for u in range(RAW_BUFS - M_TILES):
+            load_w(u)
+
+        xg = {}
+
+        def quantise_x(i):
+            nc.vector.quantize_mx(
+                out=xc[:, i, :, :].rearrange("p g m -> p (g m)").bitcast(FP8X4),
+                scales=xs[:, i, :, :].rearrange("p g m -> p (g m)"),
+                in_=xg[i][:],
+            )
+
+        def transpose_x(i, base):
+            xr = raw[("x", i)][:].bitcast(F32)
+            g = grpp.tile([P, 4096], BF16, name="grp", tag="grp", align_bytes=64)
+            xg[i] = g
+            g32 = g[:].bitcast(F32).rearrange("p (g m u) -> p g m u", g=8, u=2)
+            for bq in range(4):
+                b = base + bq
+                xt = psum.tile([P, 2, 2, P], F32, name="xt%d" % b, tag="b%d" % b)
+                for gl in range(2):
+                    for u in range(2):
+                        nc.tensor.transpose(
+                            xt[:, gl, u, :], xr[:, bq, 256 * gl + P * u : 256 * gl + P * u + P], ident[:]
+                        )
+                dst = g32[:, 2 * bq : 2 * bq + 2, :, :]
+                src = xt[:].rearrange("p g u m -> p g m u")
+                if bq < 3:
+                    nc.scalar.copy(out=dst, in_=src)
+                else:
+                    nc.vector.tensor_copy(out=dst, in_=src)
+
+        def spread_bias(base):
+            for a in range(4):
+                bb = psum.tile([P, 2 * BANK], BF16, name="bb%d" % a, tag="b%d" % (base + a))
+                for e in range(2):
+                    c = 2 * a + e
+                    nc.tensor.matmul(
+                        out=bb[:, BANK * e : BANK * e + BANK],
+                        lhsT=identb[:, c : c + 1].to_broadcast([P, P]),
+                        rhs=brow[:],
+                        start=True,
+                        stop=True,
+                    )
+                dst = bias_bc[:, 2 * BANK * a : 2 * BANK * a + 2 * BANK]
+                if a % 2 == 0:
+                    nc.scalar.copy(out=dst, in_=bb[:])
+                else:
+                    nc.vector.tensor_copy(out=dst, in_=bb[:])
+
+        transpose_x(0, 0)
+        load_w(RAW_BUFS - M_TILES)
+        transpose_x(1, 4)
+        load_w(RAW_BUFS - M_TILES + 1)
+        quantise_x(0)
+        spread_bias(0)
+        transpose_x(2, 4)
+        load_w(RAW_BUFS - M_TILES + 2)
+        quantise_x(1)
+        transpose_x(3, 0)
+        load_w(RAW_BUFS - M_TILES + 3)
+        quantise_x(2)
+
+        for s in range(n_units + 2):
+            if s < n_units:
+                regroup(s)
+                if s + RAW_BUFS < n_units:
+                    load_w(s + RAW_BUFS)
+            if s == 0:
+                quantise_x(3)
+            if 0 <= s - 1 < n_units:
+                quantise(s - 1)
+            if 0 <= s - 2 and units[s - 2][5]:
+                finish(s - 2)
+            if 0 <= s - 1 < n_units:
+                multiply(s - 1)

@@ -19,7 +19,7 @@ FLOPS = 2 * 512 * (1024 * 1024 + 2048 * 1024 + 4096 * 2048)
 
 MANUAL = True
 RAW_BUFS = 12
-ROUND_SCALAR_COLS = (896, 704, 624, 512)
+ROUND_SCALAR_COLS = (640, 640, 640, 640)
 
 
 def tile_mlinear_kernel(tc, x, w0, w1, w2, bias, out):
@@ -31,7 +31,7 @@ def tile_mlinear_kernel(tc, x, w0, w1, w2, bias, out):
         rawp = ctx.enter_context(tc.tile_pool(name="rawp", bufs=RAW_BUFS))
         grpp = ctx.enter_context(tc.tile_pool(name="grpp", bufs=4))
         wqp = ctx.enter_context(tc.tile_pool(name="wqp", bufs=4))
-        stgp = ctx.enter_context(tc.tile_pool(name="stgp", bufs=6))
+        stgp = ctx.enter_context(tc.tile_pool(name="stgp", bufs=12))
         psum = ctx.enter_context(tc.psum_pool(name="psum", bufs=1))
 
         units = []
@@ -184,10 +184,7 @@ def tile_mlinear_kernel(tc, x, w0, w1, w2, bias, out):
                         )
                 dst = g32[:, 2 * bq : 2 * bq + 2, :, :]
                 src = xt[:].rearrange("p g u m -> p g m u")
-                if bq < 3:
-                    nc.scalar.copy(out=dst, in_=src)
-                else:
-                    nc.vector.tensor_copy(out=dst, in_=src)
+                nc.scalar.copy(out=dst, in_=src)
 
         def spread_bias(base):
             for a in range(4):
@@ -202,21 +199,17 @@ def tile_mlinear_kernel(tc, x, w0, w1, w2, bias, out):
                         stop=True,
                     )
                 dst = bias_bc[:, 2 * BANK * a : 2 * BANK * a + 2 * BANK]
-                if a % 2 == 0:
-                    nc.scalar.copy(out=dst, in_=bb[:])
-                else:
-                    nc.vector.tensor_copy(out=dst, in_=bb[:])
+                nc.vector.tensor_copy(out=dst, in_=bb[:])
 
         transpose_x(0, 0)
         load_w(RAW_BUFS - M_TILES)
         transpose_x(1, 4)
         load_w(RAW_BUFS - M_TILES + 1)
         quantise_x(0)
-        spread_bias(0)
-        transpose_x(2, 4)
+        transpose_x(2, 0)
         load_w(RAW_BUFS - M_TILES + 2)
         quantise_x(1)
-        transpose_x(3, 0)
+        transpose_x(3, 4)
         load_w(RAW_BUFS - M_TILES + 3)
         quantise_x(2)
 
@@ -227,6 +220,7 @@ def tile_mlinear_kernel(tc, x, w0, w1, w2, bias, out):
                     load_w(s + RAW_BUFS)
             if s == 0:
                 quantise_x(3)
+                spread_bias(0)
             if 0 <= s - 1 < n_units:
                 quantise(s - 1)
             if 0 <= s - 2 and units[s - 2][5]:

@@ -9,6 +9,7 @@ F32 = mybir.dt.float32
 U32 = mybir.dt.uint32
 U8 = mybir.dt.uint8
 ADD = mybir.AluOpType.add
+MULT = mybir.AluOpType.mult
 
 P = 128
 M_TILES = 4
@@ -17,20 +18,20 @@ UNIT_COLS = 1024
 BANK = 512
 FLOPS = 2 * 512 * (1024 * 1024 + 2048 * 1024 + 4096 * 2048)
 
-MANUAL = True
-RAW_BUFS = 12
-ROUND_SCALAR_COLS = (640, 640, 640, 640)
+RAW_BUFS = 9
+ROUND_SCALAR_COLS = (576, 640, 704, 768)
+POOL_SHARE = True
+POOL_CUTS = (256, 480, 688, 896)
 
 
 def tile_mlinear_kernel(tc, x, w0, w1, w2, bias, out):
     nc = tc.nc
     with ExitStack() as ctx:
-        if MANUAL:
-            ctx.enter_context(tc.manual_schedule())
+        ctx.enter_context(tc.manual_schedule())
         const = ctx.enter_context(tc.tile_pool(name="const", bufs=1))
         rawp = ctx.enter_context(tc.tile_pool(name="rawp", bufs=RAW_BUFS))
-        grpp = ctx.enter_context(tc.tile_pool(name="grpp", bufs=4))
-        wqp = ctx.enter_context(tc.tile_pool(name="wqp", bufs=4))
+        grpp = ctx.enter_context(tc.tile_pool(name="grpp", bufs=5))
+        wqp = ctx.enter_context(tc.tile_pool(name="wqp", bufs=5))
         stgp = ctx.enter_context(tc.tile_pool(name="stgp", bufs=12))
         psum = ctx.enter_context(tc.psum_pool(name="psum", bufs=1))
 
@@ -44,11 +45,13 @@ def tile_mlinear_kernel(tc, x, w0, w1, w2, bias, out):
                     )
                 rnd += 1
         n_units = len(units)
+        pool_units = [u + 3 for u in range(1, n_units) if units[u][4]] if POOL_SHARE else []
 
         ident = const.tile([P, P], F32, name="ident")
         identb = const.tile([P, P], BF16, name="identb")
         brow = const.tile([P, BANK], BF16, name="brow")
         bias_bc = const.tile([P, 4096], BF16, name="bias_bc")
+        junk = const.tile([P, 8], F32, name="junk")
         xc = const.tile([P, M_TILES, 8, P], U32, name="xc", align_bytes=64)
         xs = const.tile([P, M_TILES, 8, P], U8, name="xs", align_bytes=64)
 
@@ -57,6 +60,11 @@ def tile_mlinear_kernel(tc, x, w0, w1, w2, bias, out):
         wc = {}
         ws = {}
         acc = {}
+        stg = {}
+        mark = []
+        loaded = [0]
+        held = []
+        sent = [0]
 
         def load_x(i):
             t = rawp.tile([P, 4, 1024], BF16, name="raw", tag="raw")
@@ -68,6 +76,16 @@ def tile_mlinear_kernel(tc, x, w0, w1, w2, bias, out):
             else:
                 nc.sync.dma_start(out=t[:], in_=rows)
 
+        def flush():
+            for d, s_ in held[sent[0] :]:
+                nc.sync.dma_start(out=d, in_=s_)
+            sent[0] = len(held)
+
+        def store(dst, src):
+            held.append((dst, src))
+            if loaded[0] == n_units:
+                flush()
+
         def load_w(u):
             w, c, col = units[u][0:3]
             t = rawp.tile([P, 4, 1024], BF16, name="raw", tag="raw")
@@ -78,6 +96,9 @@ def tile_mlinear_kernel(tc, x, w0, w1, w2, bias, out):
                     out=t[:, 2 * half : 2 * half + 2, :],
                     in_=w[r0 : r0 + 256, col : col + UNIT_COLS].rearrange("(q e) n -> q e n", e=2),
                 )
+            loaded[0] = u + 1
+            if loaded[0] == n_units:
+                flush()
 
         def regroup(u):
             t = raw[("w", u)]
@@ -85,13 +106,27 @@ def tile_mlinear_kernel(tc, x, w0, w1, w2, bias, out):
             grp[u] = g
             g3 = g[:].rearrange("p (n t) -> p n t", t=4)
             cs = ROUND_SCALAR_COLS[units[u][6]]
+            vs = cs
+            if u in pool_units:
+                cs = POOL_CUTS[0]
+                vs = POOL_CUTS[-1]
+                nc.gpsimd.tensor_copy(out=junk[:, 0:1], in_=mark[-1][:, 0:1])
+                for lo, hi in zip(POOL_CUTS[:-1], POOL_CUTS[1:]):
+                    nc.gpsimd.tensor_scalar(
+                        out=g3[:, lo:hi, :],
+                        in0=t[:, :, lo:hi].rearrange("p t c -> p c t"),
+                        scalar1=1.0,
+                        scalar2=0.0,
+                        op0=MULT,
+                        op1=ADD,
+                    )
             nc.scalar.copy(
                 out=g3[:, 0:cs, :].rearrange("p (c i) t -> p c t i", i=4),
                 in_=t[:, :, 0:cs].rearrange("p t (c i) -> p c t i", i=4),
             )
             nc.vector.tensor_copy(
-                out=g3[:, cs:UNIT_COLS, :].rearrange("p (c i) t -> p c t i", i=4),
-                in_=t[:, :, cs:UNIT_COLS].rearrange("p t (c i) -> p c t i", i=4),
+                out=g3[:, vs:UNIT_COLS, :].rearrange("p (c i) t -> p c t i", i=4),
+                in_=t[:, :, vs:UNIT_COLS].rearrange("p t (c i) -> p c t i", i=4),
             )
 
         def quantise(u):
@@ -113,42 +148,39 @@ def tile_mlinear_kernel(tc, x, w0, w1, w2, bias, out):
                 return [(i, j) for j in range(2) for i in range(M_TILES)]
             return [(i, j) for i in range(M_TILES) for j in range(2)]
 
-        def multiply(u):
+        def one_pass(u, i, j):
             c, first, last = units[u][1], units[u][4], units[u][5]
-            for i, j in bank_order(u):
-                b = 2 * i + j
-                if first:
-                    acc[b] = psum.tile([P, BANK], F32, name="acc%d" % b, tag="b%d" % b)
-                nc.tensor.matmul_mx(
-                    out=acc[b][:],
-                    lhsT=xc[:, i, c, :].bitcast(FP8X4),
-                    lhsT_scale=xs[:, i, c, :],
-                    rhs=wc[u][:, BANK * j : BANK * j + BANK].bitcast(FP8X4),
-                    rhs_scale=ws[u][:, BANK * j : BANK * j + BANK],
-                    start=first,
-                    stop=last,
-                )
+            b = 2 * i + j
+            if first:
+                acc[b] = psum.tile([P, BANK], F32, name="acc%d" % b, tag="b%d" % b)
+            nc.tensor.matmul_mx(
+                out=acc[b][:],
+                lhsT=xc[:, i, c, :].bitcast(FP8X4),
+                lhsT_scale=xs[:, i, c, :],
+                rhs=wc[u][:, BANK * j : BANK * j + BANK].bitcast(FP8X4),
+                rhs_scale=ws[u][:, BANK * j : BANK * j + BANK],
+                start=first,
+                stop=last,
+            )
 
-        def finish(u):
+        def empty_bank(u, i, j):
             o_col = units[u][3]
             fine = units[u][6] == rnd - 1
-            stg = {}
-            for i in range(M_TILES):
-                stg[i] = stgp.tile([P, UNIT_COLS], F32, name="stg", tag="stg")
-            for i, j in bank_order(u):
-                lo = BANK * j
-                nc.vector.tensor_tensor(
-                    out=stg[i][:, lo : lo + BANK],
-                    in0=acc[2 * i + j][:],
-                    in1=bias_bc[:, o_col + lo : o_col + lo + BANK],
-                    op=ADD,
-                )
-                if fine:
-                    nc.sync.dma_start(
-                        out=out[P * i : P * i + P, o_col + lo : o_col + lo + BANK], in_=stg[i][:, lo : lo + BANK]
-                    )
-                elif j == 1:
-                    nc.sync.dma_start(out=out[P * i : P * i + P, o_col : o_col + UNIT_COLS], in_=stg[i][:])
+            if (units[u][6], i) not in stg:
+                stg[(units[u][6], i)] = stgp.tile([P, UNIT_COLS], F32, name="stg", tag="stg")
+            st = stg[(units[u][6], i)]
+            lo = BANK * j
+            nc.vector.tensor_tensor(
+                out=st[:, lo : lo + BANK],
+                in0=acc[2 * i + j][:],
+                in1=bias_bc[:, o_col + lo : o_col + lo + BANK],
+                op=ADD,
+            )
+            if fine:
+                store(out[P * i : P * i + P, o_col + lo : o_col + lo + BANK], st[:, lo : lo + BANK])
+            elif j == 1:
+                store(out[P * i : P * i + P, o_col : o_col + UNIT_COLS], st[:])
+            return st
 
         nc.vector.memset(brow[:], 0.0)
         make_identity(nc, ident[:])
@@ -182,9 +214,7 @@ def tile_mlinear_kernel(tc, x, w0, w1, w2, bias, out):
                         nc.tensor.transpose(
                             xt[:, gl, u, :], xr[:, bq, 256 * gl + P * u : 256 * gl + P * u + P], ident[:]
                         )
-                dst = g32[:, 2 * bq : 2 * bq + 2, :, :]
-                src = xt[:].rearrange("p g u m -> p g m u")
-                nc.scalar.copy(out=dst, in_=src)
+                nc.scalar.copy(out=g32[:, 2 * bq : 2 * bq + 2, :, :], in_=xt[:].rearrange("p g u m -> p g m u"))
 
         def spread_bias(base):
             for a in range(4):
@@ -198,8 +228,7 @@ def tile_mlinear_kernel(tc, x, w0, w1, w2, bias, out):
                         start=True,
                         stop=True,
                     )
-                dst = bias_bc[:, 2 * BANK * a : 2 * BANK * a + 2 * BANK]
-                nc.vector.tensor_copy(out=dst, in_=bb[:])
+                nc.vector.tensor_copy(out=bias_bc[:, 2 * BANK * a : 2 * BANK * a + 2 * BANK], in_=bb[:])
 
         transpose_x(0, 0)
         load_w(RAW_BUFS - M_TILES)
@@ -213,7 +242,7 @@ def tile_mlinear_kernel(tc, x, w0, w1, w2, bias, out):
         load_w(RAW_BUFS - M_TILES + 3)
         quantise_x(2)
 
-        for s in range(n_units + 2):
+        for s in range(n_units + 1):
             if s < n_units:
                 regroup(s)
                 if s + RAW_BUFS < n_units:
@@ -221,9 +250,21 @@ def tile_mlinear_kernel(tc, x, w0, w1, w2, bias, out):
             if s == 0:
                 quantise_x(3)
                 spread_bias(0)
-            if 0 <= s - 1 < n_units:
-                quantise(s - 1)
-            if 0 <= s - 2 and units[s - 2][5]:
-                finish(s - 2)
-            if 0 <= s - 1 < n_units:
-                multiply(s - 1)
+                continue
+            a = s - 1
+            quantise(a)
+            pos = units[a][1]
+            if a > pos and pos == 0:
+                continue
+            if a > pos and pos == 1:
+                for n, (i, j) in enumerate(bank_order(a - 2)):
+                    st = empty_bank(a - 2, i, j)
+                    if n == 0:
+                        mark.append(st)
+                    one_pass(a - 1, i, j)
+                    one_pass(a, i, j)
+            else:
+                for i, j in bank_order(a):
+                    one_pass(a, i, j)
+        for i, j in bank_order(n_units - 1):
+            empty_bank(n_units - 1, i, j)

@@ -19,7 +19,7 @@ BANK = 512
 FLOPS = 2 * 512 * (1024 * 1024 + 2048 * 1024 + 4096 * 2048)
 
 RAW_BUFS = 9
-ROUND_SCALAR_COLS = (576, 640, 704, 768)
+ROUND_SCALAR_COLS = (384, 640, 704, 704)
 POOL_SHARE = True
 POOL_CUTS = (256, 480, 688, 896)
 
@@ -31,7 +31,7 @@ def tile_mlinear_kernel(tc, x, w0, w1, w2, bias, out):
         const = ctx.enter_context(tc.tile_pool(name="const", bufs=1))
         rawp = ctx.enter_context(tc.tile_pool(name="rawp", bufs=RAW_BUFS))
         grpp = ctx.enter_context(tc.tile_pool(name="grpp", bufs=5))
-        wqp = ctx.enter_context(tc.tile_pool(name="wqp", bufs=5))
+        wqp = ctx.enter_context(tc.tile_pool(name="wqp", bufs=6))
         stgp = ctx.enter_context(tc.tile_pool(name="stgp", bufs=12))
         psum = ctx.enter_context(tc.psum_pool(name="psum", bufs=1))
 
@@ -134,18 +134,9 @@ def tile_mlinear_kernel(tc, x, w0, w1, w2, bias, out):
             scales = wqp.tile([P, UNIT_COLS], U8, name="ws", tag="ws", align_bytes=64)
             wc[u] = codes
             ws[u] = scales
-            pieces = 2 if u == n_units - 1 else 1
-            wid = UNIT_COLS // pieces
-            for a in range(pieces):
-                nc.vector.quantize_mx(
-                    out=codes[:, wid * a : wid * a + wid].bitcast(FP8X4),
-                    scales=scales[:, wid * a : wid * a + wid],
-                    in_=grp[u][:, 4 * wid * a : 4 * wid * a + 4 * wid],
-                )
+            nc.vector.quantize_mx(out=codes[:].bitcast(FP8X4), scales=scales[:], in_=grp[u][:])
 
         def bank_order(u):
-            if units[u][6] == rnd - 1:
-                return [(i, j) for j in range(2) for i in range(M_TILES)]
             return [(i, j) for i in range(M_TILES) for j in range(2)]
 
         def one_pass(u, i, j):
@@ -232,13 +223,14 @@ def tile_mlinear_kernel(tc, x, w0, w1, w2, bias, out):
 
         transpose_x(0, 0)
         load_w(RAW_BUFS - M_TILES)
-        transpose_x(1, 4)
+        spread_bias(4)
+        transpose_x(1, 0)
         load_w(RAW_BUFS - M_TILES + 1)
         quantise_x(0)
-        transpose_x(2, 0)
+        transpose_x(2, 4)
         load_w(RAW_BUFS - M_TILES + 2)
         quantise_x(1)
-        transpose_x(3, 4)
+        transpose_x(3, 0)
         load_w(RAW_BUFS - M_TILES + 3)
         quantise_x(2)
 
@@ -249,12 +241,17 @@ def tile_mlinear_kernel(tc, x, w0, w1, w2, bias, out):
                     load_w(s + RAW_BUFS)
             if s == 0:
                 quantise_x(3)
-                spread_bias(0)
                 continue
             a = s - 1
             quantise(a)
             pos = units[a][1]
-            if a > pos and pos == 0:
+            if (a > pos and pos == 0) or a == n_units - 2:
+                continue
+            if a == n_units - 1:
+                for i, j in bank_order(a):
+                    one_pass(a - 1, i, j)
+                    one_pass(a, i, j)
+                    empty_bank(a, i, j)
                 continue
             if a > pos and pos == 1:
                 for n, (i, j) in enumerate(bank_order(a - 2)):
@@ -266,5 +263,3 @@ def tile_mlinear_kernel(tc, x, w0, w1, w2, bias, out):
             else:
                 for i, j in bank_order(a):
                     one_pass(a, i, j)
-        for i, j in bank_order(n_units - 1):
-            empty_bank(n_units - 1, i, j)

@@ -27,7 +27,6 @@ POOL_CUTS = (256, 480, 688, 896)
 def tile_mlinear_kernel(tc, x, w0, w1, w2, bias, out):
     nc = tc.nc
     with ExitStack() as ctx:
-        ctx.enter_context(tc.manual_schedule())
         const = ctx.enter_context(tc.tile_pool(name="const", bufs=1))
         rawp = ctx.enter_context(tc.tile_pool(name="rawp", bufs=RAW_BUFS))
         grpp = ctx.enter_context(tc.tile_pool(name="grpp", bufs=5))

from contextlib import ExitStack

import concourse.mybir as mybir
from concourse.masks import make_identity

FP8X4 = mybir.dt.float8_e4m3fn_x4
BF16 = mybir.dt.bfloat16
F32 = mybir.dt.float32
U32 = mybir.dt.uint32
U8 = mybir.dt.uint8
ADD = mybir.AluOpType.add
MULT = mybir.AluOpType.mult

P = 128
M_TILES = 4
K_PASS = 512
UNIT_COLS = 1024
BANK = 512
FLOPS = 2 * 512 * (1024 * 1024 + 2048 * 1024 + 4096 * 2048)

RAW_BUFS = 9
ROUND_SCALAR_COLS = (384, 640, 704, 704)
POOL_SHARE = True
POOL_CUTS = (256, 480, 688, 896)


def tile_mlinear_kernel(tc, x, w0, w1, w2, bias, out):
    nc = tc.nc
    with ExitStack() as ctx:
        const = ctx.enter_context(tc.tile_pool(name="const", bufs=1))
        rawp = ctx.enter_context(tc.tile_pool(name="rawp", bufs=RAW_BUFS))
        grpp = ctx.enter_context(tc.tile_pool(name="grpp", bufs=5))
        wqp = ctx.enter_context(tc.tile_pool(name="wqp", bufs=6))
        stgp = ctx.enter_context(tc.tile_pool(name="stgp", bufs=12))
        psum = ctx.enter_context(tc.psum_pool(name="psum", bufs=1))

        units = []
        rnd = 0
        for w, k_len, n_len, o_col in ((w0, 1024, 1024, 0), (w1, 2048, 1024, 1024), (w2, 4096, 2048, 2048)):
            for h in range(n_len // UNIT_COLS):
                for c in range(k_len // K_PASS):
                    units.append(
                        (w, c, UNIT_COLS * h, o_col + UNIT_COLS * h, c == 0, c == k_len // K_PASS - 1, rnd)
                    )
                rnd += 1
        n_units = len(units)
        pool_units = [u + 3 for u in range(1, n_units) if units[u][4]] if POOL_SHARE else []

        ident = const.tile([P, P], F32, name="ident")
        identb = const.tile([P, P], BF16, name="identb")
        brow = const.tile([P, BANK], BF16, name="brow")
        bias_bc = const.tile([P, 4096], BF16, name="bias_bc")
        junk = const.tile([P, 8], F32, name="junk")
        xc = const.tile([P, M_TILES, 8, P], U32, name="xc", align_bytes=64)
        xs = const.tile([P, M_TILES, 8, P], U8, name="xs", align_bytes=64)

        raw = {}
        grp = {}
        wc = {}
        ws = {}
        acc = {}
        stg = {}
        mark = []
        loaded = [0]
        held = []
        sent = [0]

        def load_x(i):
            t = rawp.tile([P, 4, 1024], BF16, name="raw", tag="raw")
            raw[("x", i)] = t
            rows = x[P * i : P * i + P, :].rearrange("p (b k) -> p b k", b=4)
            if i == 0:
                for b in range(4):
                    nc.sync.dma_start(out=t[:, b, :], in_=rows[:, b, :])
            else:
                nc.sync.dma_start(out=t[:], in_=rows)

        def flush():
            for d, s_ in held[sent[0] :]:
                nc.sync.dma_start(out=d, in_=s_)
            sent[0] = len(held)

        def store(dst, src):
            held.append((dst, src))
            if loaded[0] == n_units:
                flush()

        def load_w(u):
            w, c, col = units[u][0:3]
            t = rawp.tile([P, 4, 1024], BF16, name="raw", tag="raw")
            raw[("w", u)] = t
            for half in range(2):
                r0 = K_PASS * c + 256 * half
                nc.sync.dma_start(
                    out=t[:, 2 * half : 2 * half + 2, :],
                    in_=w[r0 : r0 + 256, col : col + UNIT_COLS].rearrange("(q e) n -> q e n", e=2),
                )
            loaded[0] = u + 1
            if loaded[0] == n_units:
                flush()

        def regroup(u):
            t = raw[("w", u)]
            g = grpp.tile([P, 4096], BF16, name="grp", tag="grp", align_bytes=64)
            grp[u] = g
            g3 = g[:].rearrange("p (n t) -> p n t", t=4)
            cs = ROUND_SCALAR_COLS[units[u][6]]
            vs = cs
            if u in pool_units:
                cs = POOL_CUTS[0]
                vs = POOL_CUTS[-1]
                nc.gpsimd.tensor_copy(out=junk[:, 0:1], in_=mark[-1][:, 0:1])
                for lo, hi in zip(POOL_CUTS[:-1], POOL_CUTS[1:]):
                    nc.gpsimd.tensor_scalar(
                        out=g3[:, lo:hi, :],
                        in0=t[:, :, lo:hi].rearrange("p t c -> p c t"),
                        scalar1=1.0,
                        scalar2=0.0,
                        op0=MULT,
                        op1=ADD,
                    )
            nc.scalar.copy(
                out=g3[:, 0:cs, :].rearrange("p (c i) t -> p c t i", i=4),
                in_=t[:, :, 0:cs].rearrange("p t (c i) -> p c t i", i=4),
            )
            nc.vector.tensor_copy(
                out=g3[:, vs:UNIT_COLS, :].rearrange("p (c i) t -> p c t i", i=4),
                in_=t[:, :, vs:UNIT_COLS].rearrange("p t (c i) -> p c t i", i=4),
            )

        def quantise(u):
            codes = wqp.tile([P, UNIT_COLS], U32, name="wc", tag="wc", align_bytes=64)
            scales = wqp.tile([P, UNIT_COLS], U8, name="ws", tag="ws", align_bytes=64)
            wc[u] = codes
            ws[u] = scales
            nc.vector.quantize_mx(out=codes[:].bitcast(FP8X4), scales=scales[:], in_=grp[u][:])

        def bank_order(u):
            return [(i, j) for i in range(M_TILES) for j in range(2)]

        def one_pass(u, i, j):
            c, first, last = units[u][1], units[u][4], units[u][5]
            b = 2 * i + j
            if first:
                acc[b] = psum.tile([P, BANK], F32, name="acc%d" % b, tag="b%d" % b)
            nc.tensor.matmul_mx(
                out=acc[b][:],
                lhsT=xc[:, i, c, :].bitcast(FP8X4),
                lhsT_scale=xs[:, i, c, :],
                rhs=wc[u][:, BANK * j : BANK * j + BANK].bitcast(FP8X4),
                rhs_scale=ws[u][:, BANK * j : BANK * j + BANK],
                start=first,
                stop=last,
            )

        def empty_bank(u, i, j):
            o_col = units[u][3]
            fine = units[u][6] == rnd - 1
            if (units[u][6], i) not in stg:
                stg[(units[u][6], i)] = stgp.tile([P, UNIT_COLS], F32, name="stg", tag="stg")
            st = stg[(units[u][6], i)]
            lo = BANK * j
            nc.vector.tensor_tensor(
                out=st[:, lo : lo + BANK],
                in0=acc[2 * i + j][:],
                in1=bias_bc[:, o_col + lo : o_col + lo + BANK],
                op=ADD,
            )
            if fine:
                store(out[P * i : P * i + P, o_col + lo : o_col + lo + BANK], st[:, lo : lo + BANK])
            elif j == 1:
                store(out[P * i : P * i + P, o_col : o_col + UNIT_COLS], st[:])
            return st

        nc.vector.memset(brow[:], 0.0)
        make_identity(nc, ident[:])
        make_identity(nc, identb[:])
        load_x(0)
        nc.sync.dma_start(out=brow[0:8, :], in_=bias.rearrange("(c n) -> c n", c=8))
        for i in range(1, M_TILES):
            load_x(i)
        for u in range(RAW_BUFS - M_TILES):
            load_w(u)

        xg = {}

        def quantise_x(i):
            nc.vector.quantize_mx(
                out=xc[:, i, :, :].rearrange("p g m -> p (g m)").bitcast(FP8X4),
                scales=xs[:, i, :, :].rearrange("p g m -> p (g m)"),
                in_=xg[i][:],
            )

        def transpose_x(i, base):
            xr = raw[("x", i)][:].bitcast(F32)
            g = grpp.tile([P, 4096], BF16, name="grp", tag="grp", align_bytes=64)
            xg[i] = g
            g32 = g[:].bitcast(F32).rearrange("p (g m u) -> p g m u", g=8, u=2)
            for bq in range(4):
                b = base + bq
                xt = psum.tile([P, 2, 2, P], F32, name="xt%d" % b, tag="b%d" % b)
                for gl in range(2):
                    for u in range(2):
                        nc.tensor.transpose(
                            xt[:, gl, u, :], xr[:, bq, 256 * gl + P * u : 256 * gl + P * u + P], ident[:]
                        )
                nc.scalar.copy(out=g32[:, 2 * bq : 2 * bq + 2, :, :], in_=xt[:].rearrange("p g u m -> p g m u"))

        def spread_bias(base):
            for a in range(4):
                bb = psum.tile([P, 2 * BANK], BF16, name="bb%d" % a, tag="b%d" % (base + a))
                for e in range(2):
                    c = 2 * a + e
                    nc.tensor.matmul(
                        out=bb[:, BANK * e : BANK * e + BANK],
                        lhsT=identb[:, c : c + 1].to_broadcast([P, P]),
                        rhs=brow[:],
                        start=True,
                        stop=True,
                    )
                nc.vector.tensor_copy(out=bias_bc[:, 2 * BANK * a : 2 * BANK * a + 2 * BANK], in_=bb[:])

        transpose_x(0, 0)
        load_w(RAW_BUFS - M_TILES)
        spread_bias(4)
        transpose_x(1, 0)
        load_w(RAW_BUFS - M_TILES + 1)
        quantise_x(0)
        transpose_x(2, 4)
        load_w(RAW_BUFS - M_TILES + 2)
        quantise_x(1)
        transpose_x(3, 0)
        load_w(RAW_BUFS - M_TILES + 3)
        quantise_x(2)

        for s in range(n_units + 1):
            if s < n_units:
                regroup(s)
                if s + RAW_BUFS < n_units:
                    load_w(s + RAW_BUFS)
            if s == 0:
                quantise_x(3)
                continue
            a = s - 1
            quantise(a)
            pos = units[a][1]
            if (a > pos and pos == 0) or a == n_units - 2:
                continue
            if a == n_units - 1:
                for i, j in bank_order(a):
                    one_pass(a - 1, i, j)
                    one_pass(a, i, j)
                    empty_bank(a, i, j)
                continue
            if a > pos and pos == 1:
                for n, (i, j) in enumerate(bank_order(a - 2)):
                    st = empty_bank(a - 2, i, j)
                    if n == 0:
                        mark.append(st)
                    one_pass(a - 1, i, j)
                    one_pass(a, i, j)
            else:
                for i, j in bank_order(a):
                    one_pass(a, i, j)
